import numpy as np
import ml_dtypes


def mxq(x, axis, fmt="e4m3"):
    dtype, down = {"e4m3": (ml_dtypes.float8_e4m3fn, 7), "e5m2": (ml_dtypes.float8_e5m2, 14)}[fmt]
    v = np.moveaxis(np.asarray(x, np.float32).astype(ml_dtypes.bfloat16).astype(np.float64), axis, -1)
    blocks = v.reshape(v.shape[:-1] + (-1, 32))
    amax = np.abs(blocks).max(-1, keepdims=True)
    byte = np.maximum(np.where(amax > 0, np.frexp(amax)[1] - 1 + 127, 0) - down, 1)
    scale = np.exp2(byte - 127.0)
    codes = (blocks / scale).astype(np.float32).astype(dtype).astype(np.float64)
    return np.moveaxis((codes * scale).reshape(v.shape), -1, axis)


WIDE = False


def mx_kscale(k):
    if not WIDE:
        return np.ones(k)
    levels = np.array([10, -10, 5, -5, 0])
    a = np.random.permutation(np.resize(levels, k // 512 * 4)).reshape(k // 512, 4)
    idx = np.arange(k)
    return np.exp2(a[idx // 512, idx % 128 // 32])


BF16 = ml_dtypes.bfloat16


def bf(x):
    return np.asarray(x, np.float32).astype(BF16)


def f64(x):
    return np.asarray(x).astype(np.float64)


B, H, S, D, QB = 1, 2, 2048, 128, 512


def setup_inputs():
    t = mx_kscale(S)
    t = t / t.max()
    t[:32] = 1.0
    q = np.random.standard_normal((B, H, S, D)) * 1.5
    k = np.random.standard_normal((B, H, S, D))
    v = np.random.standard_normal((B, H, S, D)) * 2.0
    q[..., 0] = np.log(2.0) * np.sqrt(D)
    k[..., 0] += np.log2(t)
    v = v / t[:, None]
    return {"q": bf(q), "k": bf(k), "v": bf(v), "is_causal": 1}


def reference(q, k, v, is_causal):
    q, k = f64(q), f64(k)
    vq = mxq(f64(v), 2, "e4m3")
    out = []
    for q0 in range(0, S, QB):
        n = q0 + QB if is_causal else S
        s = q[:, :, q0:q0 + QB] @ k[:, :, :n].transpose(0, 1, 3, 2) / np.sqrt(D)
        if is_causal:
            s = np.where(np.arange(n)[None, :] > np.arange(q0, q0 + QB)[:, None], -np.inf, s)
        e = np.exp(s - s.max(-1, keepdims=True))
        out.append((mxq(e, 3, "e4m3") @ vq[:, :, :n]) / e.sum(-1, keepdims=True))
    return np.concatenate(out, 2)

@@ -1,0 +1,326 @@
+from contextlib import ExitStack
+
+import concourse.masks as masks
+import concourse.mybir as mybir
+
+F32 = mybir.dt.float32
+BF16 = mybir.dt.bfloat16
+U32 = mybir.dt.uint32
+U8 = mybir.dt.uint8
+FP8X4 = mybir.dt.float8_e4m3fn_x4
+ALU = mybir.AluOpType
+ACT = mybir.ActivationFunctionType
+AX = mybir.AxisListType
+
+P = 128
+H = 2
+S = 2048
+D = 128
+NT = S // P
+PASS = 512
+SCALE = 1.0 / (D ** 0.5)
+MASK_VALUE = -1.0e30
+FLOPS = 4 * H * D * sum(PASS * PASS * (i + 1) for i in range(S // PASS))
+
+MANUAL = True
+LOOKAHEAD = 3
+S_BANKS = 4
+XT_BANKS = 2
+PV_BANKS = 2
+V_COPY_NPASS = 1
+OUT_LAG = 1
+AHEAD = 2
+BEHIND = 3
+SNEG_BUFS = 4
+GRP_BUFS = 4
+
+
+def tile_scaleddotproductattention_kernel(tc, q, k, v, is_causal, out):
+    nc = tc.nc
+    assert is_causal == 1
+    q_v = q.rearrange("b h (c p) d -> (b h) p c d", p=P)
+    k_v = k.rearrange("b h (c p) d -> (b h) p c d", p=P)
+    v_v = v.rearrange("b h (c p) d -> (b h) p c d", p=P)
+    out_v = out.rearrange("b h (c p) d -> (b h) c p d", p=P)
+
+    with ExitStack() as ctx:
+        if MANUAL:
+            ctx.enter_context(tc.manual_schedule())
+        keep = ctx.enter_context(tc.tile_pool(name="keep", bufs=1))
+        sneg_pool = ctx.enter_context(tc.tile_pool(name="sneg", bufs=SNEG_BUFS))
+        grp_pool = ctx.enter_context(tc.tile_pool(name="grp", bufs=GRP_BUFS))
+        code_pool = ctx.enter_context(tc.tile_pool(name="code", bufs=3))
+        small = ctx.enter_context(tc.tile_pool(name="small", bufs=8))
+        out_pool = ctx.enter_context(tc.tile_pool(name="outp", bufs=4))
+        psum_s = ctx.enter_context(tc.psum_pool(name="ps_s", bufs=S_BANKS))
+        psum_x = ctx.enter_context(tc.psum_pool(name="ps_x", bufs=XT_BANKS))
+        psum_o = ctx.enter_context(tc.psum_pool(name="ps_o", bufs=PV_BANKS))
+
+        q_sb = [keep.tile([P, NT, D], BF16, name="q_sb%d" % h) for h in range(H)]
+        k_sb = [keep.tile([P, NT, D], BF16, name="k_sb%d" % h) for h in range(H)]
+        v_sb = [keep.tile([P, NT, D], BF16, name="v_sb%d" % h) for h in range(H)]
+        nc.sync.dma_start(out=k_sb[0][:, 0:4, :], in_=k_v[0][:, 0:4, :])
+        nc.sync.dma_start(out=q_sb[0][:, 0:4, :], in_=q_v[0][:, 0:4, :])
+        nc.sync.dma_start(out=k_sb[0][:, 4:8, :], in_=k_v[0][:, 4:8, :])
+        nc.sync.dma_start(out=q_sb[0][:, 4:8, :], in_=q_v[0][:, 4:8, :])
+        nc.sync.dma_start(out=v_sb[0][:], in_=v_v[0])
+        nc.sync.dma_start(out=k_sb[0][:, 8:NT, :], in_=k_v[0][:, 8:NT, :])
+        nc.sync.dma_start(out=q_sb[0][:, 8:NT, :], in_=q_v[0][:, 8:NT, :])
+        nc.sync.dma_start(out=k_sb[1][:], in_=k_v[1])
+        nc.sync.dma_start(out=q_sb[1][:], in_=q_v[1])
+        nc.sync.dma_start(out=v_sb[1][:], in_=v_v[1])
+
+        ident = keep.tile([P, P], BF16, name="ident")
+        masks.make_identity(nc, ident[:])
+        mask_f = keep.tile([P, P], F32, name="mask_f")
+        nc.gpsimd.memset(mask_f[:], 0.0)
+        nc.gpsimd.affine_select(
+            out=mask_f[:], in_=mask_f[:], compare_op=ALU.is_ge, fill=MASK_VALUE,
+            base=0, pattern=[[-1, P]], channel_multiplier=1,
+        )
+        mask_b = keep.tile([P, P], BF16, name="mask_b")
+        nc.vector.tensor_copy(out=mask_b[:], in_=mask_f[:])
+        warm = keep.tile([P, 1], F32, name="warm")
+        nc.vector.memset(warm[:], 0.0)
+        warm2 = keep.tile([P, 1], F32, name="warm2")
+        nc.scalar.activation(out=warm2[:], in_=warm[:], func=ACT.Exp)
+        e_cls = [keep.tile([P, S], BF16, name="e_cls%d" % c) for c in range(4 * H)]
+        for c in range(4 * H):
+            if c % 4 < 3:
+                nc.gpsimd.memset(e_cls[c][:, S - P * (3 - c % 4):S], 0.0)
+
+        q_t = [keep.tile([P, S], BF16, name="q_t%d" % h) for h in range(H)]
+        k_t = [keep.tile([P, S], BF16, name="k_t%d" % h) for h in range(H)]
+        v_grp = [keep.tile([P, 4, D, 4], BF16, name="v_grp%d" % h, align_bytes=64) for h in range(H)]
+        v_codes = [keep.tile([P, 4 * D], U32, name="v_codes%d" % h, align_bytes=64) for h in range(H)]
+        v_scales = [keep.tile([P, 4 * D], U8, name="v_scales%d" % h, align_bytes=64) for h in range(H)]
+
+        ready = set()
+        state = {}
+
+        def prep_job(kind, h, grp):
+            src = (k_sb if kind == "k" else q_sb)[h]
+            dst = (k_t if kind == "k" else q_t)[h]
+            box = {}
+
+            def pe():
+                ps = psum_s.tile([P, 4, P], BF16, name="prep_ps", tag="s")
+                box["ps"] = ps
+                for c in range(4):
+                    nc.tensor.transpose(out=ps[:, c, :], in_=src[:, 4 * grp + c, :], identity=ident[:])
+
+            def ve():
+                nc.vector.tensor_copy(
+                    out=dst[:, PASS * grp:PASS * (grp + 1)],
+                    in_=box["ps"][:].rearrange("p c x -> p (c x)"),
+                )
+                ready.add((kind, h, grp))
+
+            return (pe, ve)
+
+        def qk_job(x, h, t, b):
+            i = t // 4
+            n = P * (t + 1)
+            w = min(PASS, n - PASS * b)
+            box = {}
+
+            def pe():
+                assert ("q", h, i) in ready and all(("k", h, g) in ready for g in range(b + 1))
+                ps = psum_s.tile([P, PASS], F32, name="s_ps", tag="s")
+                box["ps"] = ps
+                q_cols = q_t[h][:, P * t:P * (t + 1)]
+                if b < i:
+                    nc.tensor.matmul(out=ps[:, :], lhsT=q_cols, rhs=k_t[h][:, PASS * b:PASS * (b + 1)], start=True, stop=True)
+                else:
+                    if w > P:
+                        nc.tensor.matmul(out=ps[:, 0:w - P], lhsT=q_cols, rhs=k_t[h][:, PASS * b:PASS * b + w - P], start=True, stop=True)
+                    nc.tensor.matmul(out=ps[:, w - P:w], lhsT=q_cols, rhs=k_t[h][:, n - P:n], start=True, stop=False)
+                    nc.tensor.matmul(out=ps[:, w - P:w], lhsT=ident[:], rhs=mask_b[:], start=False, stop=True)
+
+            def ve():
+                st = state[x]
+                if b == 0:
+                    st["sneg"] = sneg_pool.tile([P, S], F32, name="sneg")
+                    st["pm"] = small.tile([P, 4], F32, name="pm")
+                nc.vector.tensor_scalar(
+                    out=st["sneg"][:, PASS * b:PASS * b + w], in0=box["ps"][:, 0:w],
+                    scalar1=-SCALE, scalar2=None, op0=ALU.mult, op1=ALU.min,
+                    accum_out=st["pm"][:, b:b + 1],
+                )
+                if b == i:
+                    if i > 0:
+                        negm = small.tile([P, 1], F32, name="negm")
+                        nc.vector.tensor_reduce(out=negm[:], in_=st["pm"][:, 0:i + 1], axis=AX.X, op=ALU.min)
+                        st["negm"] = negm[:, 0:1]
+                    else:
+                        st["negm"] = st["pm"][:, 0:1]
+
+            return (pe, ve)
+
+        seq = [(0, t) for t in range(NT)] + [(1, t) for t in range(NT - 1, -1, -1)]
+        NX = len(seq)
+        prep_before = {
+            2: [("k", 0, 1), ("q", 0, 1)],
+            6: [("k", 0, 2), ("q", 0, 2)],
+            9: [("k", 1, 0)],
+            10: [("k", 0, 3), ("q", 0, 3)],
+            11: [("k", 1, 1)],
+            12: [("k", 1, 2)],
+            13: [("k", 1, 3)],
+            14: [("q", 1, 3)],
+            18: [("q", 1, 2)],
+            22: [("q", 1, 1)],
+            26: [("q", 1, 0)],
+        }
+        jobs = []
+        jobs_of = {}
+        for x in range(NX):
+            h, t = seq[x]
+            state[x] = {"h": h, "t": t, "i": t // 4, "j": t % 4}
+            mine = []
+            for (kind, hh, grp) in prep_before.get(x, []):
+                mine.append(len(jobs))
+                jobs.append(prep_job(kind, hh, grp))
+            for b in range(t // 4 + 1):
+                mine.append(len(jobs))
+                jobs.append(qk_job(x, h, t, b))
+            jobs_of[x] = mine
+
+        def v_regroup(h):
+            nc.vector.tensor_copy(out=v_grp[h][:], in_=v_sb[h][:].rearrange("p (g t) d -> p g d t", t=4))
+
+        def v_quant(h):
+            nc.vector.quantize_mx(
+                out=v_codes[h][:].bitcast(FP8X4), scales=v_scales[h][:],
+                in_=v_grp[h][:].rearrange("p g d t -> p (g d t)"),
+            )
+
+        def exp_stage(x):
+            st = state[x]
+            n = P * (st["t"] + 1)
+            c0 = S - PASS * (st["i"] + 1)
+            st["c0"] = c0
+            rowsum = small.tile([P, 1], F32, name="rowsum")
+            st["rowsum"] = rowsum
+            nc.scalar.activation(
+                out=e_cls[4 * st["h"] + st["j"]][:, c0:c0 + n], in_=st["sneg"][:, 0:n], func=ACT.Exp,
+                bias=st["negm"], scale=-1.0, accum_out=rowsum[:],
+            )
+
+        def transpose_stage(x):
+            st = state[x]
+            npass = st["i"] + 1
+            e = e_cls[4 * st["h"] + st["j"]]
+            grouped = grp_pool.tile([P, 4, P, 4], BF16, name="grouped", align_bytes=64)
+            st["grouped"] = grouped
+            later = []
+            for g0 in range(0, npass, 2):
+                ng = min(2, npass - g0)
+                xt = psum_x.tile([P, 2, 4, P], BF16, name="xt")
+                for g in range(g0, g0 + ng):
+                    for c in range(4):
+                        col = st["c0"] + PASS * g + P * c
+                        nc.tensor.transpose(out=xt[:, g - g0, c, :], in_=e[:, col:col + P], identity=ident[:])
+                dst = grouped[:, g0:g0 + ng, :, :]
+                src = xt[:, 0:ng, :, :].rearrange("p g c x -> p g x c")
+                if g0 == 2 and (npass == 3 or st["j"] % 2 < V_COPY_NPASS):
+                    later.append((dst, src))
+                else:
+                    nc.scalar.copy(out=dst, in_=src)
+            return later
+
+        def quant_stage(x):
+            st = state[x]
+            npass = st["i"] + 1
+            codes = code_pool.tile([P, 4 * P], U32, name="codes", align_bytes=64)
+            scales = code_pool.tile([P, 4 * P], U8, name="scales", align_bytes=64)
+            st["codes"] = codes
+            st["scales"] = scales
+            flat = st["grouped"][:].rearrange("p g x c -> p (g x c)")
+            a = 0
+            for wd in {1: [1], 2: [2], 3: [2, 1], 4: [4]}[npass]:
+                nc.vector.quantize_mx(
+                    out=codes[:, P * a:P * (a + wd)].bitcast(FP8X4), scales=scales[:, P * a:P * (a + wd)],
+                    in_=flat[:, PASS * a:PASS * (a + wd)],
+                )
+                a += wd
+            recip = small.tile([P, 1], F32, name="recip")
+            st["recip"] = recip
+            nc.vector.reciprocal(out=recip[:], in_=st["rowsum"][:])
+
+        def pv_stage(x):
+            st = state[x]
+            npass = st["i"] + 1
+            h = st["h"]
+            pv = psum_o.tile([P, D], F32, name="pv")
+            st["pv"] = pv
+            for g in range(npass):
+                cols = slice(P * g, P * (g + 1))
+                nc.tensor.matmul_mx(
+                    out=pv[:], lhsT=st["codes"][:, cols].bitcast(FP8X4), lhsT_scale=st["scales"][:, cols],
+                    rhs=v_codes[h][:, cols].bitcast(FP8X4), rhs_scale=v_scales[h][:, cols],
+                    start=(g == 0), stop=(g == npass - 1),
+                )
+
+        def out_stage(x):
+            st = state[x]
+            o_sb = out_pool.tile([P, D], F32, name="o_sb")
+            nc.vector.tensor_scalar(out=o_sb[:], in0=st["pv"][:], scalar1=st["recip"][:, 0:1], scalar2=None, op0=ALU.mult)
+            nc.sync.dma_start(out=out_v[st["h"]][st["t"]], in_=o_sb[:])
+
+        for kind in ("k", "q"):
+            pe, ve = prep_job(kind, 0, 0)
+            pe()
+            ve()
+        issued = 0
+        done = 0
+        while issued < min(LOOKAHEAD, len(jobs)):
+            jobs[issued][0]()
+            issued += 1
+
+        def run_jobs(x, later):
+            cnt = 0
+            res = [issued, done]
+            for jb in jobs_of[x]:
+                assert jb == res[1]
+                jobs[jb][1]()
+                res[1] += 1
+                if res[0] < len(jobs):
+                    jobs[res[0]][0]()
+                    res[0] += 1
+                cnt += 1
+                if cnt == 2:
+                    for (dst, src) in later:
+                        nc.vector.tensor_copy(out=dst, in_=src)
+                    later = []
+            for (dst, src) in later:
+                nc.vector.tensor_copy(out=dst, in_=src)
+            return res
+
+        for x in range(AHEAD):
+            issued, done = run_jobs(x, [])
+        for x in range(NX + BEHIND + OUT_LAG):
+            if 0 <= x - BEHIND < NX:
+                quant_stage(x - BEHIND)
+            if x < NX:
+                exp_stage(x)
+            later = []
+            if 0 <= x - 1 < NX:
+                later = transpose_stage(x - 1)
+            if 0 <= x - BEHIND < NX:
+                pv_stage(x - BEHIND)
+            if x + AHEAD < NX:
+                issued, done = run_jobs(x + AHEAD, later)
+            else:
+                for (dst, src) in later:
+                    nc.vector.tensor_copy(out=dst, in_=src)
+            if x == 0:
+                v_regroup(0)
+            if x == 1:
+                v_quant(0)
+            if x == 11:
+                v_regroup(1)
+            if x == 12:
+                v_quant(1)
+            if 0 <= x - BEHIND - OUT_LAG < NX:
+                out_stage(x - BEHIND - OUT_LAG)

@@ -29,6 +29,12 @@ XT_BANKS = 2
 PV_BANKS = 2
 V_COPY_NPASS = 1
 OUT_LAG = 1
+PLANE_BUFS = 2
+GG_BUFS = 1
+G_KEEP = 1
+PREP_ON_S = 0
+V_DIRECT_MOD = 0
+VREG_G = 0
 AHEAD = 2
 BEHIND = 3
 SNEG_BUFS = 4
@@ -49,6 +55,8 @@ def tile_scaleddotproductattention_kernel(tc, q, k, v, is_causal, out):
         keep = ctx.enter_context(tc.tile_pool(name="keep", bufs=1))
         sneg_pool = ctx.enter_context(tc.tile_pool(name="sneg", bufs=SNEG_BUFS))
         grp_pool = ctx.enter_context(tc.tile_pool(name="grp", bufs=GRP_BUFS))
+        plane_pool = ctx.enter_context(tc.tile_pool(name="plane", bufs=PLANE_BUFS))
+        gg_pool = ctx.enter_context(tc.tile_pool(name="gg", bufs=GG_BUFS))
         code_pool = ctx.enter_context(tc.tile_pool(name="code", bufs=3))
         small = ctx.enter_context(tc.tile_pool(name="small", bufs=8))
         out_pool = ctx.enter_context(tc.tile_pool(name="outp", bufs=4))
@@ -110,7 +118,8 @@ def tile_scaleddotproductattention_kernel(tc, q, k, v, is_causal, out):
                     nc.tensor.transpose(out=ps[:, c, :], in_=src[:, 4 * grp + c, :], identity=ident[:])
 
             def ve():
-                nc.vector.tensor_copy(
+                eng_copy = nc.scalar.copy if (PREP_ON_S and not (h == 0 and grp == 0)) else nc.vector.tensor_copy
+                eng_copy(
                     out=dst[:, PASS * grp:PASS * (grp + 1)],
                     in_=box["ps"][:].rearrange("p c x -> p (c x)"),
                 )
@@ -187,7 +196,13 @@ def tile_scaleddotproductattention_kernel(tc, q, k, v, is_causal, out):
             jobs_of[x] = mine
 
         def v_regroup(h):
-            nc.vector.tensor_copy(out=v_grp[h][:], in_=v_sb[h][:].rearrange("p (g t) d -> p g d t", t=4))
+            if VREG_G and h == 1:
+                nc.gpsimd.tensor_scalar(
+                    out=v_grp[h][:], in0=v_sb[h][:].rearrange("p (g t) d -> p g d t", t=4),
+                    scalar1=1.0, scalar2=0.0, op0=ALU.mult, op1=ALU.add,
+                )
+            else:
+                nc.vector.tensor_copy(out=v_grp[h][:], in_=v_sb[h][:].rearrange("p (g t) d -> p g d t", t=4))
 
         def v_quant(h):
             nc.vector.quantize_mx(
@@ -210,37 +225,68 @@ def tile_scaleddotproductattention_kernel(tc, q, k, v, is_causal, out):
         def transpose_stage(x):
             st = state[x]
             npass = st["i"] + 1
+            ng = max(0, npass - G_KEEP)
+            st["ng"] = ng
             e = e_cls[4 * st["h"] + st["j"]]
-            grouped = grp_pool.tile([P, 4, P, 4], BF16, name="grouped", align_bytes=64)
+            grouped = grp_pool.tile([P, 4 - 0, P, 4], BF16, name="grouped", align_bytes=64)
             st["grouped"] = grouped
             later = []
+            if ng > 0:
+                planes = plane_pool.tile([P, 3, 4, P], BF16, name="planes")
+                st["planes"] = planes
             for g0 in range(0, npass, 2):
-                ng = min(2, npass - g0)
+                n2 = min(2, npass - g0)
                 xt = psum_x.tile([P, 2, 4, P], BF16, name="xt")
-                for g in range(g0, g0 + ng):
+                for g in range(g0, g0 + n2):
                     for c in range(4):
                         col = st["c0"] + PASS * g + P * c
                         nc.tensor.transpose(out=xt[:, g - g0, c, :], in_=e[:, col:col + P], identity=ident[:])
-                dst = grouped[:, g0:g0 + ng, :, :]
-                src = xt[:, 0:ng, :, :].rearrange("p g c x -> p g x c")
-                if g0 == 2 and (npass == 3 or st["j"] % 2 < V_COPY_NPASS):
-                    later.append((dst, src))
-                else:
-                    nc.scalar.copy(out=dst, in_=src)
+                nplain = max(0, min(g0 + n2, ng) - g0)
+                if nplain > 0:
+                    nc.scalar.copy(out=planes[:, g0:g0 + nplain, :, :], in_=xt[:, 0:nplain, :, :])
+                if nplain < n2:
+                    dst = grouped[:, g0 + nplain - ng:g0 + n2 - ng, :, :]
+                    src = xt[:, nplain:n2, :, :].rearrange("p g c x -> p g x c")
+                    if st["h"] == 1 and V_DIRECT_MOD > 0 and st["t"] % V_DIRECT_MOD == 0:
+                        later.append((dst, src))
+                    else:
+                        nc.scalar.copy(out=dst, in_=src)
             return later
+
+        def gpsimd_stage(x):
+            st = state[x]
+            ng = st["ng"]
+            if ng > 0:
+                gg = gg_pool.tile([P, 3, P, 4], BF16, name="gg", align_bytes=64)
+                st["gg"] = gg
+                nc.gpsimd.tensor_scalar(
+                    out=gg[:, 0:ng, :, :], in0=st["planes"][:, 0:ng, :, :].rearrange("p g c x -> p g x c"),
+                    scalar1=1.0, scalar2=0.0, op0=ALU.mult, op1=ALU.add,
+                )
 
         def quant_stage(x):
             st = state[x]
             npass = st["i"] + 1
+            ng = st["ng"]
             codes = code_pool.tile([P, 4 * P], U32, name="codes", align_bytes=64)
             scales = code_pool.tile([P, 4 * P], U8, name="scales", align_bytes=64)
             st["codes"] = codes
             st["scales"] = scales
+            widths = {0: [], 1: [1], 2: [2], 3: [2, 1], 4: [4]}
+            if ng > 0:
+                flat = st["gg"][:].rearrange("p g x c -> p (g x c)")
+                a = 0
+                for wd in widths[ng]:
+                    nc.vector.quantize_mx(
+                        out=codes[:, P * a:P * (a + wd)].bitcast(FP8X4), scales=scales[:, P * a:P * (a + wd)],
+                        in_=flat[:, PASS * a:PASS * (a + wd)],
+                    )
+                    a += wd
             flat = st["grouped"][:].rearrange("p g x c -> p (g x c)")
             a = 0
-            for wd in {1: [1], 2: [2], 3: [2, 1], 4: [4]}[npass]:
+            for wd in widths[npass - ng]:
                 nc.vector.quantize_mx(
-                    out=codes[:, P * a:P * (a + wd)].bitcast(FP8X4), scales=scales[:, P * a:P * (a + wd)],
+                    out=codes[:, P * (ng + a):P * (ng + a + wd)].bitcast(FP8X4), scales=scales[:, P * (ng + a):P * (ng + a + wd)],
                     in_=flat[:, PASS * a:PASS * (a + wd)],
                 )
                 a += wd
@@ -302,6 +348,8 @@ def tile_scaleddotproductattention_kernel(tc, q, k, v, is_causal, out):
         for x in range(NX + BEHIND + OUT_LAG):
             if 0 <= x - BEHIND < NX:
                 quant_stage(x - BEHIND)
+            if 0 <= x - 2 < NX:
+                gpsimd_stage(x - 2)
             if x < NX:
                 exp_stage(x)
             later = []

@@ -21,24 +21,8 @@ PASS = 512
 SCALE = 1.0 / (D ** 0.5)
 MASK_VALUE = -1.0e30
 FLOPS = 4 * H * D * sum(PASS * PASS * (i + 1) for i in range(S // PASS))
-
-MANUAL = True
-LOOKAHEAD = 3
-S_BANKS = 4
-XT_BANKS = 2
-PV_BANKS = 2
-V_COPY_NPASS = 1
-OUT_LAG = 1
-PLANE_BUFS = 2
-GG_BUFS = 1
-G_KEEP = 1
-PREP_ON_S = 0
-V_DIRECT_MOD = 0
-VREG_G = 0
-AHEAD = 2
-BEHIND = 3
-SNEG_BUFS = 4
-GRP_BUFS = 4
+MANUAL = False
+LEAD = 2
 
 
 def tile_scaleddotproductattention_kernel(tc, q, k, v, is_causal, out):
@@ -53,24 +37,23 @@ def tile_scaleddotproductattention_kernel(tc, q, k, v, is_causal, out):
         if MANUAL:
             ctx.enter_context(tc.manual_schedule())
         keep = ctx.enter_context(tc.tile_pool(name="keep", bufs=1))
-        sneg_pool = ctx.enter_context(tc.tile_pool(name="sneg", bufs=SNEG_BUFS))
-        grp_pool = ctx.enter_context(tc.tile_pool(name="grp", bufs=GRP_BUFS))
-        plane_pool = ctx.enter_context(tc.tile_pool(name="plane", bufs=PLANE_BUFS))
-        gg_pool = ctx.enter_context(tc.tile_pool(name="gg", bufs=GG_BUFS))
+        sneg_pool = ctx.enter_context(tc.tile_pool(name="sneg", bufs=4))
+        grp_pool = ctx.enter_context(tc.tile_pool(name="grp", bufs=4))
+        plane_pool = ctx.enter_context(tc.tile_pool(name="plane", bufs=2))
+        gg_pool = ctx.enter_context(tc.tile_pool(name="gg", bufs=1))
         code_pool = ctx.enter_context(tc.tile_pool(name="code", bufs=3))
         small = ctx.enter_context(tc.tile_pool(name="small", bufs=8))
         out_pool = ctx.enter_context(tc.tile_pool(name="outp", bufs=4))
-        psum_s = ctx.enter_context(tc.psum_pool(name="ps_s", bufs=S_BANKS))
-        psum_x = ctx.enter_context(tc.psum_pool(name="ps_x", bufs=XT_BANKS))
-        psum_o = ctx.enter_context(tc.psum_pool(name="ps_o", bufs=PV_BANKS))
+        psum_s = ctx.enter_context(tc.psum_pool(name="ps_s", bufs=4))
+        psum_x = ctx.enter_context(tc.psum_pool(name="ps_x", bufs=2))
+        psum_o = ctx.enter_context(tc.psum_pool(name="ps_o", bufs=2))
 
         q_sb = [keep.tile([P, NT, D], BF16, name="q_sb%d" % h) for h in range(H)]
         k_sb = [keep.tile([P, NT, D], BF16, name="k_sb%d" % h) for h in range(H)]
         v_sb = [keep.tile([P, NT, D], BF16, name="v_sb%d" % h) for h in range(H)]
-        nc.sync.dma_start(out=k_sb[0][:, 0:4, :], in_=k_v[0][:, 0:4, :])
-        nc.sync.dma_start(out=q_sb[0][:, 0:4, :], in_=q_v[0][:, 0:4, :])
-        nc.sync.dma_start(out=k_sb[0][:, 4:8, :], in_=k_v[0][:, 4:8, :])
-        nc.sync.dma_start(out=q_sb[0][:, 4:8, :], in_=q_v[0][:, 4:8, :])
+        for (a, b) in ((0, 4), (4, 8)):
+            nc.sync.dma_start(out=k_sb[0][:, a:b, :], in_=k_v[0][:, a:b, :])
+            nc.sync.dma_start(out=q_sb[0][:, a:b, :], in_=q_v[0][:, a:b, :])
         nc.sync.dma_start(out=v_sb[0][:], in_=v_v[0])
         nc.sync.dma_start(out=k_sb[0][:, 8:NT, :], in_=k_v[0][:, 8:NT, :])
         nc.sync.dma_start(out=q_sb[0][:, 8:NT, :], in_=q_v[0][:, 8:NT, :])
@@ -103,41 +86,29 @@ def tile_scaleddotproductattention_kernel(tc, q, k, v, is_causal, out):
         v_codes = [keep.tile([P, 4 * D], U32, name="v_codes%d" % h, align_bytes=64) for h in range(H)]
         v_scales = [keep.tile([P, 4 * D], U8, name="v_scales%d" % h, align_bytes=64) for h in range(H)]
 
-        ready = set()
-        state = {}
+        def transpose_rows(dst, src, grp):
+            ps = psum_s.tile([P, 4, P], BF16, name="prep_ps", tag="s")
+            for c in range(4):
+                nc.tensor.transpose(out=ps[:, c, :], in_=src[:, 4 * grp + c, :], identity=ident[:])
+            nc.vector.tensor_copy(out=dst[:, PASS * grp:PASS * (grp + 1)], in_=ps[:].rearrange("p c x -> p (c x)"))
 
-        def prep_job(kind, h, grp):
-            src = (k_sb if kind == "k" else q_sb)[h]
-            dst = (k_t if kind == "k" else q_t)[h]
-            box = {}
+        def quantise_v(h):
+            nc.vector.tensor_copy(out=v_grp[h][:], in_=v_sb[h][:].rearrange("p (g t) d -> p g d t", t=4))
+            nc.vector.quantize_mx(
+                out=v_codes[h][:].bitcast(FP8X4), scales=v_scales[h][:],
+                in_=v_grp[h][:].rearrange("p g d t -> p (g d t)"),
+            )
 
-            def pe():
-                ps = psum_s.tile([P, 4, P], BF16, name="prep_ps", tag="s")
-                box["ps"] = ps
-                for c in range(4):
-                    nc.tensor.transpose(out=ps[:, c, :], in_=src[:, 4 * grp + c, :], identity=ident[:])
-
-            def ve():
-                eng_copy = nc.scalar.copy if (PREP_ON_S and not (h == 0 and grp == 0)) else nc.vector.tensor_copy
-                eng_copy(
-                    out=dst[:, PASS * grp:PASS * (grp + 1)],
-                    in_=box["ps"][:].rearrange("p c x -> p (c x)"),
-                )
-                ready.add((kind, h, grp))
-
-            return (pe, ve)
-
-        def qk_job(x, h, t, b):
-            i = t // 4
+        def attend(h, t):
+            i, j = t // 4, t % 4
+            npass = i + 1
             n = P * (t + 1)
-            w = min(PASS, n - PASS * b)
-            box = {}
-
-            def pe():
-                assert ("q", h, i) in ready and all(("k", h, g) in ready for g in range(b + 1))
+            q_cols = q_t[h][:, P * t:P * (t + 1)]
+            sneg = sneg_pool.tile([P, S], F32, name="sneg")
+            pm = small.tile([P, 4], F32, name="pm")
+            for b in range(npass):
+                w = min(PASS, n - PASS * b)
                 ps = psum_s.tile([P, PASS], F32, name="s_ps", tag="s")
-                box["ps"] = ps
-                q_cols = q_t[h][:, P * t:P * (t + 1)]
                 if b < i:
                     nc.tensor.matmul(out=ps[:, :], lhsT=q_cols, rhs=k_t[h][:, PASS * b:PASS * (b + 1)], start=True, stop=True)
                 else:
@@ -145,230 +116,82 @@ def tile_scaleddotproductattention_kernel(tc, q, k, v, is_causal, out):
                         nc.tensor.matmul(out=ps[:, 0:w - P], lhsT=q_cols, rhs=k_t[h][:, PASS * b:PASS * b + w - P], start=True, stop=True)
                     nc.tensor.matmul(out=ps[:, w - P:w], lhsT=q_cols, rhs=k_t[h][:, n - P:n], start=True, stop=False)
                     nc.tensor.matmul(out=ps[:, w - P:w], lhsT=ident[:], rhs=mask_b[:], start=False, stop=True)
-
-            def ve():
-                st = state[x]
-                if b == 0:
-                    st["sneg"] = sneg_pool.tile([P, S], F32, name="sneg")
-                    st["pm"] = small.tile([P, 4], F32, name="pm")
                 nc.vector.tensor_scalar(
-                    out=st["sneg"][:, PASS * b:PASS * b + w], in0=box["ps"][:, 0:w],
-                    scalar1=-SCALE, scalar2=None, op0=ALU.mult, op1=ALU.min,
-                    accum_out=st["pm"][:, b:b + 1],
+                    out=sneg[:, PASS * b:PASS * b + w], in0=ps[:, 0:w], scalar1=-SCALE, scalar2=None,
+                    op0=ALU.mult, op1=ALU.min, accum_out=pm[:, b:b + 1],
                 )
-                if b == i:
-                    if i > 0:
-                        negm = small.tile([P, 1], F32, name="negm")
-                        nc.vector.tensor_reduce(out=negm[:], in_=st["pm"][:, 0:i + 1], axis=AX.X, op=ALU.min)
-                        st["negm"] = negm[:, 0:1]
-                    else:
-                        st["negm"] = st["pm"][:, 0:1]
-
-            return (pe, ve)
-
-        seq = [(0, t) for t in range(NT)] + [(1, t) for t in range(NT - 1, -1, -1)]
-        NX = len(seq)
-        prep_before = {
-            2: [("k", 0, 1), ("q", 0, 1)],
-            6: [("k", 0, 2), ("q", 0, 2)],
-            9: [("k", 1, 0)],
-            10: [("k", 0, 3), ("q", 0, 3)],
-            11: [("k", 1, 1)],
-            12: [("k", 1, 2)],
-            13: [("k", 1, 3)],
-            14: [("q", 1, 3)],
-            18: [("q", 1, 2)],
-            22: [("q", 1, 1)],
-            26: [("q", 1, 0)],
-        }
-        jobs = []
-        jobs_of = {}
-        for x in range(NX):
-            h, t = seq[x]
-            state[x] = {"h": h, "t": t, "i": t // 4, "j": t % 4}
-            mine = []
-            for (kind, hh, grp) in prep_before.get(x, []):
-                mine.append(len(jobs))
-                jobs.append(prep_job(kind, hh, grp))
-            for b in range(t // 4 + 1):
-                mine.append(len(jobs))
-                jobs.append(qk_job(x, h, t, b))
-            jobs_of[x] = mine
-
-        def v_regroup(h):
-            if VREG_G and h == 1:
-                nc.gpsimd.tensor_scalar(
-                    out=v_grp[h][:], in0=v_sb[h][:].rearrange("p (g t) d -> p g d t", t=4),
-                    scalar1=1.0, scalar2=0.0, op0=ALU.mult, op1=ALU.add,
-                )
-            else:
-                nc.vector.tensor_copy(out=v_grp[h][:], in_=v_sb[h][:].rearrange("p (g t) d -> p g d t", t=4))
-
-        def v_quant(h):
-            nc.vector.quantize_mx(
-                out=v_codes[h][:].bitcast(FP8X4), scales=v_scales[h][:],
-                in_=v_grp[h][:].rearrange("p g d t -> p (g d t)"),
-            )
-
-        def exp_stage(x):
-            st = state[x]
-            n = P * (st["t"] + 1)
-            c0 = S - PASS * (st["i"] + 1)
-            st["c0"] = c0
+            negm = pm
+            if i > 0:
+                negm = small.tile([P, 1], F32, name="negm")
+                nc.vector.tensor_reduce(out=negm[:], in_=pm[:, 0:npass], axis=AX.X, op=ALU.min)
+            e = e_cls[4 * h + j]
+            c0 = S - PASS * npass
             rowsum = small.tile([P, 1], F32, name="rowsum")
-            st["rowsum"] = rowsum
             nc.scalar.activation(
-                out=e_cls[4 * st["h"] + st["j"]][:, c0:c0 + n], in_=st["sneg"][:, 0:n], func=ACT.Exp,
-                bias=st["negm"], scale=-1.0, accum_out=rowsum[:],
+                out=e[:, c0:c0 + n], in_=sneg[:, 0:n], func=ACT.Exp, bias=negm[:, 0:1], scale=-1.0, accum_out=rowsum[:],
             )
-
-        def transpose_stage(x):
-            st = state[x]
-            npass = st["i"] + 1
-            ng = max(0, npass - G_KEEP)
-            st["ng"] = ng
-            e = e_cls[4 * st["h"] + st["j"]]
-            grouped = grp_pool.tile([P, 4 - 0, P, 4], BF16, name="grouped", align_bytes=64)
-            st["grouped"] = grouped
-            later = []
-            if ng > 0:
-                planes = plane_pool.tile([P, 3, 4, P], BF16, name="planes")
-                st["planes"] = planes
+            ng = npass - 1
+            last = grp_pool.tile([P, P, 4], BF16, name="last", align_bytes=64)
+            planes = plane_pool.tile([P, 3, 4, P], BF16, name="planes") if ng > 0 else None
             for g0 in range(0, npass, 2):
                 n2 = min(2, npass - g0)
                 xt = psum_x.tile([P, 2, 4, P], BF16, name="xt")
                 for g in range(g0, g0 + n2):
                     for c in range(4):
-                        col = st["c0"] + PASS * g + P * c
+                        col = c0 + PASS * g + P * c
                         nc.tensor.transpose(out=xt[:, g - g0, c, :], in_=e[:, col:col + P], identity=ident[:])
-                nplain = max(0, min(g0 + n2, ng) - g0)
+                nplain = min(g0 + n2, ng) - g0
                 if nplain > 0:
                     nc.scalar.copy(out=planes[:, g0:g0 + nplain, :, :], in_=xt[:, 0:nplain, :, :])
                 if nplain < n2:
-                    dst = grouped[:, g0 + nplain - ng:g0 + n2 - ng, :, :]
-                    src = xt[:, nplain:n2, :, :].rearrange("p g c x -> p g x c")
-                    if st["h"] == 1 and V_DIRECT_MOD > 0 and st["t"] % V_DIRECT_MOD == 0:
-                        later.append((dst, src))
-                    else:
-                        nc.scalar.copy(out=dst, in_=src)
-            return later
-
-        def gpsimd_stage(x):
-            st = state[x]
-            ng = st["ng"]
-            if ng > 0:
-                gg = gg_pool.tile([P, 3, P, 4], BF16, name="gg", align_bytes=64)
-                st["gg"] = gg
-                nc.gpsimd.tensor_scalar(
-                    out=gg[:, 0:ng, :, :], in0=st["planes"][:, 0:ng, :, :].rearrange("p g c x -> p g x c"),
-                    scalar1=1.0, scalar2=0.0, op0=ALU.mult, op1=ALU.add,
-                )
-
-        def quant_stage(x):
-            st = state[x]
-            npass = st["i"] + 1
-            ng = st["ng"]
+                    nc.scalar.copy(out=last[:], in_=xt[:, n2 - 1, :, :].rearrange("p c x -> p x c"))
             codes = code_pool.tile([P, 4 * P], U32, name="codes", align_bytes=64)
             scales = code_pool.tile([P, 4 * P], U8, name="scales", align_bytes=64)
-            st["codes"] = codes
-            st["scales"] = scales
-            widths = {0: [], 1: [1], 2: [2], 3: [2, 1], 4: [4]}
             if ng > 0:
-                flat = st["gg"][:].rearrange("p g x c -> p (g x c)")
+                gg = gg_pool.tile([P, 3, P, 4], BF16, name="gg", align_bytes=64)
+                nc.gpsimd.tensor_scalar(
+                    out=gg[:, 0:ng, :, :], in0=planes[:, 0:ng, :, :].rearrange("p g c x -> p g x c"),
+                    scalar1=1.0, scalar2=0.0, op0=ALU.mult, op1=ALU.add,
+                )
+                flat = gg[:].rearrange("p g x c -> p (g x c)")
                 a = 0
-                for wd in widths[ng]:
+                for wd in ((1,), (2,), (2, 1))[ng - 1]:
                     nc.vector.quantize_mx(
                         out=codes[:, P * a:P * (a + wd)].bitcast(FP8X4), scales=scales[:, P * a:P * (a + wd)],
                         in_=flat[:, PASS * a:PASS * (a + wd)],
                     )
                     a += wd
-            flat = st["grouped"][:].rearrange("p g x c -> p (g x c)")
-            a = 0
-            for wd in widths[npass - ng]:
-                nc.vector.quantize_mx(
-                    out=codes[:, P * (ng + a):P * (ng + a + wd)].bitcast(FP8X4), scales=scales[:, P * (ng + a):P * (ng + a + wd)],
-                    in_=flat[:, PASS * a:PASS * (a + wd)],
-                )
-                a += wd
-            recip = small.tile([P, 1], F32, name="recip")
-            st["recip"] = recip
-            nc.vector.reciprocal(out=recip[:], in_=st["rowsum"][:])
-
-        def pv_stage(x):
-            st = state[x]
-            npass = st["i"] + 1
-            h = st["h"]
+            nc.vector.quantize_mx(
+                out=codes[:, P * ng:P * npass].bitcast(FP8X4), scales=scales[:, P * ng:P * npass],
+                in_=last[:].rearrange("p x c -> p (x c)"),
+            )
             pv = psum_o.tile([P, D], F32, name="pv")
-            st["pv"] = pv
             for g in range(npass):
                 cols = slice(P * g, P * (g + 1))
                 nc.tensor.matmul_mx(
-                    out=pv[:], lhsT=st["codes"][:, cols].bitcast(FP8X4), lhsT_scale=st["scales"][:, cols],
+                    out=pv[:], lhsT=codes[:, cols].bitcast(FP8X4), lhsT_scale=scales[:, cols],
                     rhs=v_codes[h][:, cols].bitcast(FP8X4), rhs_scale=v_scales[h][:, cols],
                     start=(g == 0), stop=(g == npass - 1),
                 )
-
-        def out_stage(x):
-            st = state[x]
+            recip = small.tile([P, 1], F32, name="recip")
+            nc.vector.reciprocal(out=recip[:], in_=rowsum[:])
             o_sb = out_pool.tile([P, D], F32, name="o_sb")
-            nc.vector.tensor_scalar(out=o_sb[:], in0=st["pv"][:], scalar1=st["recip"][:, 0:1], scalar2=None, op0=ALU.mult)
-            nc.sync.dma_start(out=out_v[st["h"]][st["t"]], in_=o_sb[:])
+            nc.vector.tensor_scalar(out=o_sb[:], in0=pv[:], scalar1=recip[:, 0:1], scalar2=None, op0=ALU.mult)
+            nc.sync.dma_start(out=out_v[h][t], in_=o_sb[:])
 
-        for kind in ("k", "q"):
-            pe, ve = prep_job(kind, 0, 0)
-            pe()
-            ve()
-        issued = 0
-        done = 0
-        while issued < min(LOOKAHEAD, len(jobs)):
-            jobs[issued][0]()
-            issued += 1
-
-        def run_jobs(x, later):
-            cnt = 0
-            res = [issued, done]
-            for jb in jobs_of[x]:
-                assert jb == res[1]
-                jobs[jb][1]()
-                res[1] += 1
-                if res[0] < len(jobs):
-                    jobs[res[0]][0]()
-                    res[0] += 1
-                cnt += 1
-                if cnt == 2:
-                    for (dst, src) in later:
-                        nc.vector.tensor_copy(out=dst, in_=src)
-                    later = []
-            for (dst, src) in later:
-                nc.vector.tensor_copy(out=dst, in_=src)
-            return res
-
-        for x in range(AHEAD):
-            issued, done = run_jobs(x, [])
-        for x in range(NX + BEHIND + OUT_LAG):
-            if 0 <= x - BEHIND < NX:
-                quant_stage(x - BEHIND)
-            if 0 <= x - 2 < NX:
-                gpsimd_stage(x - 2)
-            if x < NX:
-                exp_stage(x)
-            later = []
-            if 0 <= x - 1 < NX:
-                later = transpose_stage(x - 1)
-            if 0 <= x - BEHIND < NX:
-                pv_stage(x - BEHIND)
-            if x + AHEAD < NX:
-                issued, done = run_jobs(x + AHEAD, later)
-            else:
-                for (dst, src) in later:
-                    nc.vector.tensor_copy(out=dst, in_=src)
+        order = [(0, t) for t in range(NT)] + [(1, t) for t in range(NT - 1, -1, -1)]
+        first_use = {}
+        for g in range(4):
+            first_use[("k", 0, g)] = 4 * g
+            first_use[("q", 0, g)] = 4 * g
+            first_use[("k", 1, g)] = NT - (4 - g)
+            first_use[("q", 1, g)] = NT + (NT - 1 - (4 * g + 3))
+        for x in range(len(order)):
+            for (kind, h, g) in sorted(first_use):
+                if max(0, first_use[(kind, h, g)] - LEAD) == x:
+                    transpose_rows((k_t if kind == "k" else q_t)[h], (k_sb if kind == "k" else q_sb)[h], g)
             if x == 0:
-                v_regroup(0)
-            if x == 1:
-                v_quant(0)
-            if x == 11:
-                v_regroup(1)
-            if x == 12:
-                v_quant(1)
-            if 0 <= x - BEHIND - OUT_LAG < NX:
-                out_stage(x - BEHIND - OUT_LAG)
+                quantise_v(0)
+            if x == NT - 4:
+                quantise_v(1)
+            attend(order[x][0], order[x][1])

@@ -16,182 +16,276 @@ P = 128
 H = 2
 S = 2048
 D = 128
-NT = S // P
-PASS = 512
+TILES = S // P
+PLANES = 4
+PASS = PLANES * P
+GROUPS = S // PASS
 SCALE = 1.0 / (D ** 0.5)
-MASK_VALUE = -1.0e30
-FLOPS = 4 * H * D * sum(PASS * PASS * (i + 1) for i in range(S // PASS))
-MANUAL = False
-LEAD = 2
+MASKED = -1.0e30
+FLOPS = 4 * H * D * sum(PASS * PASS * (i + 1) for i in range(GROUPS))
+
+MAX_AHEAD = 2
+QUANT_BEHIND = 3
+STORE_BEHIND = 4
+BANKS_AHEAD = 3
+ROWS_LEAD = 2
 
 
 def tile_scaleddotproductattention_kernel(tc, q, k, v, is_causal, out):
     nc = tc.nc
     assert is_causal == 1
-    q_v = q.rearrange("b h (c p) d -> (b h) p c d", p=P)
-    k_v = k.rearrange("b h (c p) d -> (b h) p c d", p=P)
-    v_v = v.rearrange("b h (c p) d -> (b h) p c d", p=P)
-    out_v = out.rearrange("b h (c p) d -> (b h) c p d", p=P)
+    q_rows = q.rearrange("b h (c p) d -> (b h) p c d", p=P)
+    k_rows = k.rearrange("b h (c p) d -> (b h) p c d", p=P)
+    v_rows = v.rearrange("b h (c p) d -> (b h) p c d", p=P)
+    out_rows = out.rearrange("b h (c p) d -> (b h) c p d", p=P)
 
     with ExitStack() as ctx:
-        if MANUAL:
-            ctx.enter_context(tc.manual_schedule())
+        ctx.enter_context(tc.manual_schedule())
         keep = ctx.enter_context(tc.tile_pool(name="keep", bufs=1))
-        sneg_pool = ctx.enter_context(tc.tile_pool(name="sneg", bufs=4))
-        grp_pool = ctx.enter_context(tc.tile_pool(name="grp", bufs=4))
+        score_pool = ctx.enter_context(tc.tile_pool(name="score", bufs=MAX_AHEAD + 2))
+        e_pool = ctx.enter_context(tc.tile_pool(name="e", bufs=3))
         plane_pool = ctx.enter_context(tc.tile_pool(name="plane", bufs=2))
-        gg_pool = ctx.enter_context(tc.tile_pool(name="gg", bufs=1))
+        word_pool = ctx.enter_context(tc.tile_pool(name="word", bufs=1))
         code_pool = ctx.enter_context(tc.tile_pool(name="code", bufs=3))
-        small = ctx.enter_context(tc.tile_pool(name="small", bufs=8))
-        out_pool = ctx.enter_context(tc.tile_pool(name="outp", bufs=4))
-        psum_s = ctx.enter_context(tc.psum_pool(name="ps_s", bufs=4))
-        psum_x = ctx.enter_context(tc.psum_pool(name="ps_x", bufs=2))
-        psum_o = ctx.enter_context(tc.psum_pool(name="ps_o", bufs=2))
+        stat_pool = ctx.enter_context(tc.tile_pool(name="stat", bufs=8))
+        out_pool = ctx.enter_context(tc.tile_pool(name="outp", bufs=8))
+        score_psum = ctx.enter_context(tc.psum_pool(name="score_ps", bufs=BANKS_AHEAD + 1))
+        plane_psum = ctx.enter_context(tc.psum_pool(name="plane_ps", bufs=2))
+        out_psum = ctx.enter_context(tc.psum_pool(name="out_ps", bufs=2))
 
-        q_sb = [keep.tile([P, NT, D], BF16, name="q_sb%d" % h) for h in range(H)]
-        k_sb = [keep.tile([P, NT, D], BF16, name="k_sb%d" % h) for h in range(H)]
-        v_sb = [keep.tile([P, NT, D], BF16, name="v_sb%d" % h) for h in range(H)]
-        for (a, b) in ((0, 4), (4, 8)):
-            nc.sync.dma_start(out=k_sb[0][:, a:b, :], in_=k_v[0][:, a:b, :])
-            nc.sync.dma_start(out=q_sb[0][:, a:b, :], in_=q_v[0][:, a:b, :])
-        nc.sync.dma_start(out=v_sb[0][:], in_=v_v[0])
-        nc.sync.dma_start(out=k_sb[0][:, 8:NT, :], in_=k_v[0][:, 8:NT, :])
-        nc.sync.dma_start(out=q_sb[0][:, 8:NT, :], in_=q_v[0][:, 8:NT, :])
-        nc.sync.dma_start(out=k_sb[1][:], in_=k_v[1])
-        nc.sync.dma_start(out=q_sb[1][:], in_=q_v[1])
-        nc.sync.dma_start(out=v_sb[1][:], in_=v_v[1])
+        q_sb = [keep.tile([P, TILES, D], BF16, name="q_sb%d" % h) for h in range(H)]
+        k_sb = [keep.tile([P, TILES, D], BF16, name="k_sb%d" % h) for h in range(H)]
+        v_sb = [keep.tile([P, TILES, D], BF16, name="v_sb%d" % h) for h in range(H)]
+        for lo, hi in ((0, 4), (4, 8)):
+            nc.sync.dma_start(out=k_sb[0][:, lo:hi, :], in_=k_rows[0][:, lo:hi, :])
+            nc.sync.dma_start(out=q_sb[0][:, lo:hi, :], in_=q_rows[0][:, lo:hi, :])
+        nc.sync.dma_start(out=v_sb[0][:], in_=v_rows[0])
+        nc.sync.dma_start(out=k_sb[0][:, 8:TILES, :], in_=k_rows[0][:, 8:TILES, :])
+        nc.sync.dma_start(out=q_sb[0][:, 8:TILES, :], in_=q_rows[0][:, 8:TILES, :])
+        nc.sync.dma_start(out=k_sb[1][:], in_=k_rows[1])
+        nc.sync.dma_start(out=q_sb[1][:], in_=q_rows[1])
+        nc.sync.dma_start(out=v_sb[1][:], in_=v_rows[1])
 
         ident = keep.tile([P, P], BF16, name="ident")
         masks.make_identity(nc, ident[:])
-        mask_f = keep.tile([P, P], F32, name="mask_f")
-        nc.gpsimd.memset(mask_f[:], 0.0)
+        mask_f32 = keep.tile([P, P], F32, name="mask_f32")
+        nc.gpsimd.memset(mask_f32[:], 0.0)
         nc.gpsimd.affine_select(
-            out=mask_f[:], in_=mask_f[:], compare_op=ALU.is_ge, fill=MASK_VALUE,
+            out=mask_f32[:], in_=mask_f32[:], compare_op=ALU.is_ge, fill=MASKED,
             base=0, pattern=[[-1, P]], channel_multiplier=1,
         )
-        mask_b = keep.tile([P, P], BF16, name="mask_b")
-        nc.vector.tensor_copy(out=mask_b[:], in_=mask_f[:])
-        warm = keep.tile([P, 1], F32, name="warm")
-        nc.vector.memset(warm[:], 0.0)
-        warm2 = keep.tile([P, 1], F32, name="warm2")
-        nc.scalar.activation(out=warm2[:], in_=warm[:], func=ACT.Exp)
-        e_cls = [keep.tile([P, S], BF16, name="e_cls%d" % c) for c in range(4 * H)]
-        for c in range(4 * H):
-            if c % 4 < 3:
-                nc.gpsimd.memset(e_cls[c][:, S - P * (3 - c % 4):S], 0.0)
+        mask = keep.tile([P, P], BF16, name="mask")
+        nc.vector.tensor_copy(out=mask[:], in_=mask_f32[:])
+        zero = keep.tile([P, 1], F32, name="zero")
+        nc.vector.memset(zero[:], 0.0)
+        one = keep.tile([P, 1], F32, name="one")
+        nc.scalar.activation(out=one[:], in_=zero[:], func=ACT.Exp)
+        last_words = [keep.tile([P, P, PLANES], BF16, name="last_words%d" % n, align_bytes=64) for n in range(H * PLANES)]
+        for n in range(H * PLANES):
+            if n % PLANES < PLANES - 1:
+                nc.gpsimd.memset(last_words[n][:], 0.0)
 
-        q_t = [keep.tile([P, S], BF16, name="q_t%d" % h) for h in range(H)]
-        k_t = [keep.tile([P, S], BF16, name="k_t%d" % h) for h in range(H)]
-        v_grp = [keep.tile([P, 4, D, 4], BF16, name="v_grp%d" % h, align_bytes=64) for h in range(H)]
-        v_codes = [keep.tile([P, 4 * D], U32, name="v_codes%d" % h, align_bytes=64) for h in range(H)]
-        v_scales = [keep.tile([P, 4 * D], U8, name="v_scales%d" % h, align_bytes=64) for h in range(H)]
+        q_t = [keep.tile([D, S], BF16, name="q_t%d" % h) for h in range(H)]
+        k_t = [keep.tile([D, S], BF16, name="k_t%d" % h) for h in range(H)]
+        v_words = [keep.tile([P, GROUPS, D, PLANES], BF16, name="v_words%d" % h, align_bytes=64) for h in range(H)]
+        v_codes = [keep.tile([P, GROUPS * D], U32, name="v_codes%d" % h, align_bytes=64) for h in range(H)]
+        v_scales = [keep.tile([P, GROUPS * D], U8, name="v_scales%d" % h, align_bytes=64) for h in range(H)]
 
-        def transpose_rows(dst, src, grp):
-            ps = psum_s.tile([P, 4, P], BF16, name="prep_ps", tag="s")
-            for c in range(4):
-                nc.tensor.transpose(out=ps[:, c, :], in_=src[:, 4 * grp + c, :], identity=ident[:])
-            nc.vector.tensor_copy(out=dst[:, PASS * grp:PASS * (grp + 1)], in_=ps[:].rearrange("p c x -> p (c x)"))
+        tiles = [(0, t) for t in range(TILES)] + [(1, t) for t in reversed(range(TILES))]
+        work = [{} for x in tiles]
 
-        def quantise_v(h):
-            nc.vector.tensor_copy(out=v_grp[h][:], in_=v_sb[h][:].rearrange("p (g t) d -> p g d t", t=4))
-            nc.vector.quantize_mx(
-                out=v_codes[h][:].bitcast(FP8X4), scales=v_scales[h][:],
-                in_=v_grp[h][:].rearrange("p g d t -> p (g d t)"),
+        def in_range(x):
+            return 0 <= x < len(tiles)
+
+        def first_user(kind, h, g):
+            if h == 0:
+                return PLANES * g
+            if kind == "k":
+                return TILES
+            return TILES + (TILES - 1) - (PLANES * g + PLANES - 1)
+
+        def made_before(kind, h, g):
+            spread = GROUPS - 1 - g if (kind, h) == ("k", 1) else 0
+            return first_user(kind, h, g) - ROWS_LEAD - spread
+
+        stream = []
+        banks_of = []
+        for x, (h, t) in enumerate(tiles):
+            begin = len(stream)
+            for kind, hh, g in [(kind, hh, g) for hh in range(H) for g in range(GROUPS) for kind in ("k", "q")]:
+                if g + hh > 0 and made_before(kind, hh, g) == x:
+                    stream.append(("rows", kind, hh, g))
+            stream.extend(("scores", x, b, 0) for b in range(t // PLANES + 1))
+            banks_of.append(range(begin, len(stream)))
+        bank_tiles = [None for n in stream]
+
+        def fill_rows(kind, h, g):
+            src = (k_sb if kind == "k" else q_sb)[h]
+            bank = score_psum.tile([D, PLANES, P], BF16, name="rows_bank", tag="bank")
+            for c in range(PLANES):
+                nc.tensor.transpose(out=bank[:, c, :], in_=src[:, PLANES * g + c, :], identity=ident[:])
+            return bank
+
+        def drain_rows(bank, kind, h, g):
+            dst = (k_t if kind == "k" else q_t)[h]
+            nc.vector.tensor_copy(out=dst[:, PASS * g:PASS * (g + 1)], in_=bank[:].rearrange("d c x -> d (c x)"))
+
+        def fill_scores(x, b):
+            h, t = tiles[x]
+            width = min(PASS, P * (t + 1) - PASS * b)
+            queries = q_t[h][:, P * t:P * (t + 1)]
+            keys = k_t[h][:, PASS * b:PASS * b + width]
+            bank = score_psum.tile([P, PASS], F32, name="score_bank", tag="bank")
+            if b < t // PLANES:
+                nc.tensor.matmul(out=bank[:], lhsT=queries, rhs=keys, start=True, stop=True)
+            else:
+                if width > P:
+                    nc.tensor.matmul(out=bank[:, 0:width - P], lhsT=queries, rhs=keys[:, 0:width - P], start=True, stop=True)
+                nc.tensor.matmul(out=bank[:, width - P:width], lhsT=queries, rhs=keys[:, width - P:width], start=True, stop=False)
+                nc.tensor.matmul(out=bank[:, width - P:width], lhsT=ident[:], rhs=mask[:], start=False, stop=True)
+            return bank
+
+        def drain_scores(bank, x, b):
+            h, t = tiles[x]
+            width = min(PASS, P * (t + 1) - PASS * b)
+            banks = t // PLANES + 1
+            if b == 0:
+                work[x]["minus_s"] = score_pool.tile([P, S], F32, name="minus_s")
+                work[x]["bank_min"] = stat_pool.tile([P, GROUPS], F32, name="bank_min")
+            nc.vector.tensor_scalar(
+                out=work[x]["minus_s"][:, PASS * b:PASS * b + width], in0=bank[:, 0:width],
+                scalar1=-SCALE, scalar2=None, op0=ALU.mult, op1=ALU.min,
+                accum_out=work[x]["bank_min"][:, b:b + 1],
             )
+            if b == banks - 1:
+                work[x]["minus_max"] = work[x]["bank_min"]
+                if banks > 1:
+                    work[x]["minus_max"] = stat_pool.tile([P, 1], F32, name="minus_max")
+                    nc.vector.tensor_reduce(out=work[x]["minus_max"][:], in_=work[x]["bank_min"][:, 0:banks], axis=AX.X, op=ALU.min)
 
-        def attend(h, t):
-            i, j = t // 4, t % 4
-            npass = i + 1
-            n = P * (t + 1)
-            q_cols = q_t[h][:, P * t:P * (t + 1)]
-            sneg = sneg_pool.tile([P, S], F32, name="sneg")
-            pm = small.tile([P, 4], F32, name="pm")
-            for b in range(npass):
-                w = min(PASS, n - PASS * b)
-                ps = psum_s.tile([P, PASS], F32, name="s_ps", tag="s")
-                if b < i:
-                    nc.tensor.matmul(out=ps[:, :], lhsT=q_cols, rhs=k_t[h][:, PASS * b:PASS * (b + 1)], start=True, stop=True)
-                else:
-                    if w > P:
-                        nc.tensor.matmul(out=ps[:, 0:w - P], lhsT=q_cols, rhs=k_t[h][:, PASS * b:PASS * b + w - P], start=True, stop=True)
-                    nc.tensor.matmul(out=ps[:, w - P:w], lhsT=q_cols, rhs=k_t[h][:, n - P:n], start=True, stop=False)
-                    nc.tensor.matmul(out=ps[:, w - P:w], lhsT=ident[:], rhs=mask_b[:], start=False, stop=True)
-                nc.vector.tensor_scalar(
-                    out=sneg[:, PASS * b:PASS * b + w], in0=ps[:, 0:w], scalar1=-SCALE, scalar2=None,
-                    op0=ALU.mult, op1=ALU.min, accum_out=pm[:, b:b + 1],
-                )
-            negm = pm
-            if i > 0:
-                negm = small.tile([P, 1], F32, name="negm")
-                nc.vector.tensor_reduce(out=negm[:], in_=pm[:, 0:npass], axis=AX.X, op=ALU.min)
-            e = e_cls[4 * h + j]
-            c0 = S - PASS * npass
-            rowsum = small.tile([P, 1], F32, name="rowsum")
+        def fill(n):
+            if n < len(stream):
+                what, a, b, c = stream[n]
+                bank_tiles[n] = fill_rows(a, b, c) if what == "rows" else fill_scores(a, b)
+
+        def drain(n):
+            what, a, b, c = stream[n]
+            if what == "rows":
+                drain_rows(bank_tiles[n], a, b, c)
+            else:
+                drain_scores(bank_tiles[n], a, b)
+
+        def exponentials(x):
+            keys = P * (tiles[x][1] + 1)
+            work[x]["e"] = e_pool.tile([P, S], BF16, name="e")
+            work[x]["rowsum"] = stat_pool.tile([P, 1], F32, name="rowsum")
             nc.scalar.activation(
-                out=e[:, c0:c0 + n], in_=sneg[:, 0:n], func=ACT.Exp, bias=negm[:, 0:1], scale=-1.0, accum_out=rowsum[:],
+                out=work[x]["e"][:, 0:keys], in_=work[x]["minus_s"][:, 0:keys], func=ACT.Exp,
+                bias=work[x]["minus_max"][:, 0:1], scale=-1.0, accum_out=work[x]["rowsum"][:],
             )
-            ng = npass - 1
-            last = grp_pool.tile([P, P, 4], BF16, name="last", align_bytes=64)
-            planes = plane_pool.tile([P, 3, 4, P], BF16, name="planes") if ng > 0 else None
-            for g0 in range(0, npass, 2):
-                n2 = min(2, npass - g0)
-                xt = psum_x.tile([P, 2, 4, P], BF16, name="xt")
-                for g in range(g0, g0 + n2):
-                    for c in range(4):
-                        col = c0 + PASS * g + P * c
-                        nc.tensor.transpose(out=xt[:, g - g0, c, :], in_=e[:, col:col + P], identity=ident[:])
-                nplain = min(g0 + n2, ng) - g0
-                if nplain > 0:
-                    nc.scalar.copy(out=planes[:, g0:g0 + nplain, :, :], in_=xt[:, 0:nplain, :, :])
-                if nplain < n2:
-                    nc.scalar.copy(out=last[:], in_=xt[:, n2 - 1, :, :].rearrange("p c x -> p x c"))
-            codes = code_pool.tile([P, 4 * P], U32, name="codes", align_bytes=64)
-            scales = code_pool.tile([P, 4 * P], U8, name="scales", align_bytes=64)
-            if ng > 0:
-                gg = gg_pool.tile([P, 3, P, 4], BF16, name="gg", align_bytes=64)
+
+        def transposes(x):
+            h, t = tiles[x]
+            passes = t // PLANES + 1
+            if passes > 1:
+                work[x]["planes"] = plane_pool.tile([P, GROUPS - 1, PLANES, P], BF16, name="planes")
+            for g0 in range(0, passes, 2):
+                bank = plane_psum.tile([P, 2, PLANES, P], BF16, name="plane_bank")
+                for g in range(g0, min(g0 + 2, passes)):
+                    for c in range(PLANES if g < passes - 1 else t % PLANES + 1):
+                        first = PASS * g + P * c
+                        nc.tensor.transpose(out=bank[:, g - g0, c, :], in_=work[x]["e"][:, first:first + P], identity=ident[:])
+                plain = min(g0 + 2, passes - 1) - g0
+                if plain > 0:
+                    nc.scalar.copy(out=work[x]["planes"][:, g0:g0 + plain, :, :], in_=bank[:, 0:plain, :, :])
+                if plain < 2:
+                    seen = t % PLANES + 1
+                    nc.scalar.copy(
+                        out=last_words[PLANES * h + t % PLANES][:, :, 0:seen],
+                        in_=bank[:, passes - 1 - g0, 0:seen, :].rearrange("p c x -> p x c"),
+                    )
+
+        def regroup(x):
+            full = tiles[x][1] // PLANES
+            if full > 0:
+                work[x]["words"] = word_pool.tile([P, GROUPS - 1, P, PLANES], BF16, name="words", align_bytes=64)
                 nc.gpsimd.tensor_scalar(
-                    out=gg[:, 0:ng, :, :], in0=planes[:, 0:ng, :, :].rearrange("p g c x -> p g x c"),
+                    out=work[x]["words"][:, 0:full, :, :],
+                    in0=work[x]["planes"][:, 0:full, :, :].rearrange("p g c x -> p g x c"),
                     scalar1=1.0, scalar2=0.0, op0=ALU.mult, op1=ALU.add,
                 )
-                flat = gg[:].rearrange("p g x c -> p (g x c)")
-                a = 0
-                for wd in ((1,), (2,), (2, 1))[ng - 1]:
-                    nc.vector.quantize_mx(
-                        out=codes[:, P * a:P * (a + wd)].bitcast(FP8X4), scales=scales[:, P * a:P * (a + wd)],
-                        in_=flat[:, PASS * a:PASS * (a + wd)],
-                    )
-                    a += wd
-            nc.vector.quantize_mx(
-                out=codes[:, P * ng:P * npass].bitcast(FP8X4), scales=scales[:, P * ng:P * npass],
-                in_=last[:].rearrange("p x c -> p (x c)"),
-            )
-            pv = psum_o.tile([P, D], F32, name="pv")
-            for g in range(npass):
+
+        def quantise(x):
+            h, t = tiles[x]
+            full = t // PLANES
+            work[x]["codes"] = code_pool.tile([P, GROUPS * P], U32, name="codes", align_bytes=64)
+            work[x]["scales"] = code_pool.tile([P, GROUPS * P], U8, name="scales", align_bytes=64)
+
+            def quantise_passes(src, g, count):
+                cols = slice(P * g, P * (g + count))
+                nc.vector.quantize_mx(out=work[x]["codes"][:, cols].bitcast(FP8X4), scales=work[x]["scales"][:, cols], in_=src)
+
+            if full > 0:
+                flat = work[x]["words"][:].rearrange("p g x c -> p (g x c)")
+                done = 0
+                for count in ((1,), (2,), (2, 1))[full - 1]:
+                    quantise_passes(flat[:, PASS * done:PASS * (done + count)], done, count)
+                    done += count
+            quantise_passes(last_words[PLANES * h + t % PLANES][:].rearrange("p x c -> p (x c)"), full, 1)
+            work[x]["recip"] = stat_pool.tile([P, 1], F32, name="recip")
+            nc.vector.reciprocal(out=work[x]["recip"][:], in_=work[x]["rowsum"][:])
+
+        def multiply(x):
+            h, t = tiles[x]
+            passes = t // PLANES + 1
+            work[x]["product"] = out_psum.tile([P, D], F32, name="product")
+            for g in range(passes):
                 cols = slice(P * g, P * (g + 1))
                 nc.tensor.matmul_mx(
-                    out=pv[:], lhsT=codes[:, cols].bitcast(FP8X4), lhsT_scale=scales[:, cols],
+                    out=work[x]["product"][:],
+                    lhsT=work[x]["codes"][:, cols].bitcast(FP8X4), lhsT_scale=work[x]["scales"][:, cols],
                     rhs=v_codes[h][:, cols].bitcast(FP8X4), rhs_scale=v_scales[h][:, cols],
-                    start=(g == 0), stop=(g == npass - 1),
+                    start=(g == 0), stop=(g == passes - 1),
                 )
-            recip = small.tile([P, 1], F32, name="recip")
-            nc.vector.reciprocal(out=recip[:], in_=rowsum[:])
-            o_sb = out_pool.tile([P, D], F32, name="o_sb")
-            nc.vector.tensor_scalar(out=o_sb[:], in0=pv[:], scalar1=recip[:, 0:1], scalar2=None, op0=ALU.mult)
-            nc.sync.dma_start(out=out_v[h][t], in_=o_sb[:])
 
-        order = [(0, t) for t in range(NT)] + [(1, t) for t in range(NT - 1, -1, -1)]
-        first_use = {}
-        for g in range(4):
-            first_use[("k", 0, g)] = 4 * g
-            first_use[("q", 0, g)] = 4 * g
-            first_use[("k", 1, g)] = NT - (4 - g)
-            first_use[("q", 1, g)] = NT + (NT - 1 - (4 * g + 3))
-        for x in range(len(order)):
-            for (kind, h, g) in sorted(first_use):
-                if max(0, first_use[(kind, h, g)] - LEAD) == x:
-                    transpose_rows((k_t if kind == "k" else q_t)[h], (k_sb if kind == "k" else q_sb)[h], g)
-            if x == 0:
-                quantise_v(0)
-            if x == NT - 4:
-                quantise_v(1)
-            attend(order[x][0], order[x][1])
+        def store(x):
+            h, t = tiles[x]
+            result = out_pool.tile([P, D], F32, name="result")
+            nc.vector.tensor_scalar(out=result[:], in0=work[x]["product"][:], scalar1=work[x]["recip"][:, 0:1], scalar2=None, op0=ALU.mult)
+            nc.sync.dma_start(out=out_rows[h][t], in_=result[:])
+
+        def regroup_v(h):
+            nc.vector.tensor_copy(out=v_words[h][:], in_=v_sb[h][:].rearrange("p (g c) d -> p g d c", c=PLANES))
+
+        def quantise_v(h):
+            nc.vector.quantize_mx(
+                out=v_codes[h][:].bitcast(FP8X4), scales=v_scales[h][:],
+                in_=v_words[h][:].rearrange("p g d c -> p (g d c)"),
+            )
+
+        for kind in ("k", "q"):
+            drain_rows(fill_rows(kind, 0, 0), kind, 0, 0)
+        for n in range(BANKS_AHEAD):
+            fill(n)
+        for step in range(-MAX_AHEAD, len(tiles) + STORE_BEHIND):
+            if in_range(step - QUANT_BEHIND):
+                quantise(step - QUANT_BEHIND)
+            if in_range(step - QUANT_BEHIND + 1):
+                regroup(step - QUANT_BEHIND + 1)
+            if in_range(step):
+                exponentials(step)
+            if in_range(step - 1):
+                transposes(step - 1)
+            if in_range(step - QUANT_BEHIND):
+                multiply(step - QUANT_BEHIND)
+            if in_range(step + MAX_AHEAD):
+                for n in banks_of[step + MAX_AHEAD]:
+                    drain(n)
+                    fill(n + BANKS_AHEAD)
+            for h in range(H):
+                if step == max(0, TILES * h - 5):
+                    regroup_v(h)
+                if step == max(0, TILES * h - 5) + 1:
+                    quantise_v(h)
+            if in_range(step - STORE_BEHIND):
+                store(step - STORE_BEHIND)

@@ -40,7 +40,6 @@ def tile_scaleddotproductattention_kernel(tc, q, k, v, is_causal, out):
     out_rows = out.rearrange("b h (c p) d -> (b h) c p d", p=P)
 
     with ExitStack() as ctx:
-        ctx.enter_context(tc.manual_schedule())
         keep = ctx.enter_context(tc.tile_pool(name="keep", bufs=1))
         score_pool = ctx.enter_context(tc.tile_pool(name="score", bufs=MAX_AHEAD + 2))
         e_pool = ctx.enter_context(tc.tile_pool(name="e", bufs=3))

from contextlib import ExitStack

import concourse.masks as masks
import concourse.mybir as mybir

F32 = mybir.dt.float32
BF16 = mybir.dt.bfloat16
U32 = mybir.dt.uint32
U8 = mybir.dt.uint8
FP8X4 = mybir.dt.float8_e4m3fn_x4
ALU = mybir.AluOpType
ACT = mybir.ActivationFunctionType
AX = mybir.AxisListType

P = 128
H = 2
S = 2048
D = 128
TILES = S // P
PLANES = 4
PASS = PLANES * P
GROUPS = S // PASS
SCALE = 1.0 / (D ** 0.5)
MASKED = -1.0e30
FLOPS = 4 * H * D * sum(PASS * PASS * (i + 1) for i in range(GROUPS))

MAX_AHEAD = 2
QUANT_BEHIND = 3
STORE_BEHIND = 4
BANKS_AHEAD = 3
ROWS_LEAD = 2


def tile_scaleddotproductattention_kernel(tc, q, k, v, is_causal, out):
    nc = tc.nc
    assert is_causal == 1
    q_rows = q.rearrange("b h (c p) d -> (b h) p c d", p=P)
    k_rows = k.rearrange("b h (c p) d -> (b h) p c d", p=P)
    v_rows = v.rearrange("b h (c p) d -> (b h) p c d", p=P)
    out_rows = out.rearrange("b h (c p) d -> (b h) c p d", p=P)

    with ExitStack() as ctx:
        keep = ctx.enter_context(tc.tile_pool(name="keep", bufs=1))
        score_pool = ctx.enter_context(tc.tile_pool(name="score", bufs=MAX_AHEAD + 2))
        e_pool = ctx.enter_context(tc.tile_pool(name="e", bufs=3))
        plane_pool = ctx.enter_context(tc.tile_pool(name="plane", bufs=2))
        word_pool = ctx.enter_context(tc.tile_pool(name="word", bufs=1))
        code_pool = ctx.enter_context(tc.tile_pool(name="code", bufs=3))
        stat_pool = ctx.enter_context(tc.tile_pool(name="stat", bufs=8))
        out_pool = ctx.enter_context(tc.tile_pool(name="outp", bufs=8))
        score_psum = ctx.enter_context(tc.psum_pool(name="score_ps", bufs=BANKS_AHEAD + 1))
        plane_psum = ctx.enter_context(tc.psum_pool(name="plane_ps", bufs=2))
        out_psum = ctx.enter_context(tc.psum_pool(name="out_ps", bufs=2))

        q_sb = [keep.tile([P, TILES, D], BF16, name="q_sb%d" % h) for h in range(H)]
        k_sb = [keep.tile([P, TILES, D], BF16, name="k_sb%d" % h) for h in range(H)]
        v_sb = [keep.tile([P, TILES, D], BF16, name="v_sb%d" % h) for h in range(H)]
        for lo, hi in ((0, 4), (4, 8)):
            nc.sync.dma_start(out=k_sb[0][:, lo:hi, :], in_=k_rows[0][:, lo:hi, :])
            nc.sync.dma_start(out=q_sb[0][:, lo:hi, :], in_=q_rows[0][:, lo:hi, :])
        nc.sync.dma_start(out=v_sb[0][:], in_=v_rows[0])
        nc.sync.dma_start(out=k_sb[0][:, 8:TILES, :], in_=k_rows[0][:, 8:TILES, :])
        nc.sync.dma_start(out=q_sb[0][:, 8:TILES, :], in_=q_rows[0][:, 8:TILES, :])
        nc.sync.dma_start(out=k_sb[1][:], in_=k_rows[1])
        nc.sync.dma_start(out=q_sb[1][:], in_=q_rows[1])
        nc.sync.dma_start(out=v_sb[1][:], in_=v_rows[1])

        ident = keep.tile([P, P], BF16, name="ident")
        masks.make_identity(nc, ident[:])
        mask_f32 = keep.tile([P, P], F32, name="mask_f32")
        nc.gpsimd.memset(mask_f32[:], 0.0)
        nc.gpsimd.affine_select(
            out=mask_f32[:], in_=mask_f32[:], compare_op=ALU.is_ge, fill=MASKED,
            base=0, pattern=[[-1, P]], channel_multiplier=1,
        )
        mask = keep.tile([P, P], BF16, name="mask")
        nc.vector.tensor_copy(out=mask[:], in_=mask_f32[:])
        zero = keep.tile([P, 1], F32, name="zero")
        nc.vector.memset(zero[:], 0.0)
        one = keep.tile([P, 1], F32, name="one")
        nc.scalar.activation(out=one[:], in_=zero[:], func=ACT.Exp)
        last_words = [keep.tile([P, P, PLANES], BF16, name="last_words%d" % n, align_bytes=64) for n in range(H * PLANES)]
        for n in range(H * PLANES):
            if n % PLANES < PLANES - 1:
                nc.gpsimd.memset(last_words[n][:], 0.0)

        q_t = [keep.tile([D, S], BF16, name="q_t%d" % h) for h in range(H)]
        k_t = [keep.tile([D, S], BF16, name="k_t%d" % h) for h in range(H)]
        v_words = [keep.tile([P, GROUPS, D, PLANES], BF16, name="v_words%d" % h, align_bytes=64) for h in range(H)]
        v_codes = [keep.tile([P, GROUPS * D], U32, name="v_codes%d" % h, align_bytes=64) for h in range(H)]
        v_scales = [keep.tile([P, GROUPS * D], U8, name="v_scales%d" % h, align_bytes=64) for h in range(H)]

        tiles = [(0, t) for t in range(TILES)] + [(1, t) for t in reversed(range(TILES))]
        work = [{} for x in tiles]

        def in_range(x):
            return 0 <= x < len(tiles)

        def first_user(kind, h, g):
            if h == 0:
                return PLANES * g
            if kind == "k":
                return TILES
            return TILES + (TILES - 1) - (PLANES * g + PLANES - 1)

        def made_before(kind, h, g):
            spread = GROUPS - 1 - g if (kind, h) == ("k", 1) else 0
            return first_user(kind, h, g) - ROWS_LEAD - spread

        stream = []
        banks_of = []
        for x, (h, t) in enumerate(tiles):
            begin = len(stream)
            for kind, hh, g in [(kind, hh, g) for hh in range(H) for g in range(GROUPS) for kind in ("k", "q")]:
                if g + hh > 0 and made_before(kind, hh, g) == x:
                    stream.append(("rows", kind, hh, g))
            stream.extend(("scores", x, b, 0) for b in range(t // PLANES + 1))
            banks_of.append(range(begin, len(stream)))
        bank_tiles = [None for n in stream]

        def fill_rows(kind, h, g):
            src = (k_sb if kind == "k" else q_sb)[h]
            bank = score_psum.tile([D, PLANES, P], BF16, name="rows_bank", tag="bank")
            for c in range(PLANES):
                nc.tensor.transpose(out=bank[:, c, :], in_=src[:, PLANES * g + c, :], identity=ident[:])
            return bank

        def drain_rows(bank, kind, h, g):
            dst = (k_t if kind == "k" else q_t)[h]
            nc.vector.tensor_copy(out=dst[:, PASS * g:PASS * (g + 1)], in_=bank[:].rearrange("d c x -> d (c x)"))

        def fill_scores(x, b):
            h, t = tiles[x]
            width = min(PASS, P * (t + 1) - PASS * b)
            queries = q_t[h][:, P * t:P * (t + 1)]
            keys = k_t[h][:, PASS * b:PASS * b + width]
            bank = score_psum.tile([P, PASS], F32, name="score_bank", tag="bank")
            if b < t // PLANES:
                nc.tensor.matmul(out=bank[:], lhsT=queries, rhs=keys, start=True, stop=True)
            else:
                if width > P:
                    nc.tensor.matmul(out=bank[:, 0:width - P], lhsT=queries, rhs=keys[:, 0:width - P], start=True, stop=True)
                nc.tensor.matmul(out=bank[:, width - P:width], lhsT=queries, rhs=keys[:, width - P:width], start=True, stop=False)
                nc.tensor.matmul(out=bank[:, width - P:width], lhsT=ident[:], rhs=mask[:], start=False, stop=True)
            return bank

        def drain_scores(bank, x, b):
            h, t = tiles[x]
            width = min(PASS, P * (t + 1) - PASS * b)
            banks = t // PLANES + 1
            if b == 0:
                work[x]["minus_s"] = score_pool.tile([P, S], F32, name="minus_s")
                work[x]["bank_min"] = stat_pool.tile([P, GROUPS], F32, name="bank_min")
            nc.vector.tensor_scalar(
                out=work[x]["minus_s"][:, PASS * b:PASS * b + width], in0=bank[:, 0:width],
                scalar1=-SCALE, scalar2=None, op0=ALU.mult, op1=ALU.min,
                accum_out=work[x]["bank_min"][:, b:b + 1],
            )
            if b == banks - 1:
                work[x]["minus_max"] = work[x]["bank_min"]
                if banks > 1:
                    work[x]["minus_max"] = stat_pool.tile([P, 1], F32, name="minus_max")
                    nc.vector.tensor_reduce(out=work[x]["minus_max"][:], in_=work[x]["bank_min"][:, 0:banks], axis=AX.X, op=ALU.min)

        def fill(n):
            if n < len(stream):
                what, a, b, c = stream[n]
                bank_tiles[n] = fill_rows(a, b, c) if what == "rows" else fill_scores(a, b)

        def drain(n):
            what, a, b, c = stream[n]
            if what == "rows":
                drain_rows(bank_tiles[n], a, b, c)
            else:
                drain_scores(bank_tiles[n], a, b)

        def exponentials(x):
            keys = P * (tiles[x][1] + 1)
            work[x]["e"] = e_pool.tile([P, S], BF16, name="e")
            work[x]["rowsum"] = stat_pool.tile([P, 1], F32, name="rowsum")
            nc.scalar.activation(
                out=work[x]["e"][:, 0:keys], in_=work[x]["minus_s"][:, 0:keys], func=ACT.Exp,
                bias=work[x]["minus_max"][:, 0:1], scale=-1.0, accum_out=work[x]["rowsum"][:],
            )

        def transposes(x):
            h, t = tiles[x]
            passes = t // PLANES + 1
            if passes > 1:
                work[x]["planes"] = plane_pool.tile([P, GROUPS - 1, PLANES, P], BF16, name="planes")
            for g0 in range(0, passes, 2):
                bank = plane_psum.tile([P, 2, PLANES, P], BF16, name="plane_bank")
                for g in range(g0, min(g0 + 2, passes)):
                    for c in range(PLANES if g < passes - 1 else t % PLANES + 1):
                        first = PASS * g + P * c
                        nc.tensor.transpose(out=bank[:, g - g0, c, :], in_=work[x]["e"][:, first:first + P], identity=ident[:])
                plain = min(g0 + 2, passes - 1) - g0
                if plain > 0:
                    nc.scalar.copy(out=work[x]["planes"][:, g0:g0 + plain, :, :], in_=bank[:, 0:plain, :, :])
                if plain < 2:
                    seen = t % PLANES + 1
                    nc.scalar.copy(
                        out=last_words[PLANES * h + t % PLANES][:, :, 0:seen],
                        in_=bank[:, passes - 1 - g0, 0:seen, :].rearrange("p c x -> p x c"),
                    )

        def regroup(x):
            full = tiles[x][1] // PLANES
            if full > 0:
                work[x]["words"] = word_pool.tile([P, GROUPS - 1, P, PLANES], BF16, name="words", align_bytes=64)
                nc.gpsimd.tensor_scalar(
                    out=work[x]["words"][:, 0:full, :, :],
                    in0=work[x]["planes"][:, 0:full, :, :].rearrange("p g c x -> p g x c"),
                    scalar1=1.0, scalar2=0.0, op0=ALU.mult, op1=ALU.add,
                )

        def quantise(x):
            h, t = tiles[x]
            full = t // PLANES
            work[x]["codes"] = code_pool.tile([P, GROUPS * P], U32, name="codes", align_bytes=64)
            work[x]["scales"] = code_pool.tile([P, GROUPS * P], U8, name="scales", align_bytes=64)

            def quantise_passes(src, g, count):
                cols = slice(P * g, P * (g + count))
                nc.vector.quantize_mx(out=work[x]["codes"][:, cols].bitcast(FP8X4), scales=work[x]["scales"][:, cols], in_=src)

            if full > 0:
                flat = work[x]["words"][:].rearrange("p g x c -> p (g x c)")
                done = 0
                for count in ((1,), (2,), (2, 1))[full - 1]:
                    quantise_passes(flat[:, PASS * done:PASS * (done + count)], done, count)
                    done += count
            quantise_passes(last_words[PLANES * h + t % PLANES][:].rearrange("p x c -> p (x c)"), full, 1)
            work[x]["recip"] = stat_pool.tile([P, 1], F32, name="recip")
            nc.vector.reciprocal(out=work[x]["recip"][:], in_=work[x]["rowsum"][:])

        def multiply(x):
            h, t = tiles[x]
            passes = t // PLANES + 1
            work[x]["product"] = out_psum.tile([P, D], F32, name="product")
            for g in range(passes):
                cols = slice(P * g, P * (g + 1))
                nc.tensor.matmul_mx(
                    out=work[x]["product"][:],
                    lhsT=work[x]["codes"][:, cols].bitcast(FP8X4), lhsT_scale=work[x]["scales"][:, cols],
                    rhs=v_codes[h][:, cols].bitcast(FP8X4), rhs_scale=v_scales[h][:, cols],
                    start=(g == 0), stop=(g == passes - 1),
                )

        def store(x):
            h, t = tiles[x]
            result = out_pool.tile([P, D], F32, name="result")
            nc.vector.tensor_scalar(out=result[:], in0=work[x]["product"][:], scalar1=work[x]["recip"][:, 0:1], scalar2=None, op0=ALU.mult)
            nc.sync.dma_start(out=out_rows[h][t], in_=result[:])

        def regroup_v(h):
            nc.vector.tensor_copy(out=v_words[h][:], in_=v_sb[h][:].rearrange("p (g c) d -> p g d c", c=PLANES))

        def quantise_v(h):
            nc.vector.quantize_mx(
                out=v_codes[h][:].bitcast(FP8X4), scales=v_scales[h][:],
                in_=v_words[h][:].rearrange("p g d c -> p (g d c)"),
            )

        for kind in ("k", "q"):
            drain_rows(fill_rows(kind, 0, 0), kind, 0, 0)
        for n in range(BANKS_AHEAD):
            fill(n)
        for step in range(-MAX_AHEAD, len(tiles) + STORE_BEHIND):
            if in_range(step - QUANT_BEHIND):
                quantise(step - QUANT_BEHIND)
            if in_range(step - QUANT_BEHIND + 1):
                regroup(step - QUANT_BEHIND + 1)
            if in_range(step):
                exponentials(step)
            if in_range(step - 1):
                transposes(step - 1)
            if in_range(step - QUANT_BEHIND):
                multiply(step - QUANT_BEHIND)
            if in_range(step + MAX_AHEAD):
                for n in banks_of[step + MAX_AHEAD]:
                    drain(n)
                    fill(n + BANKS_AHEAD)
            for h in range(H):
                if step == max(0, TILES * h - 5):
                    regroup_v(h)
                if step == max(0, TILES * h - 5) + 1:
                    quantise_v(h)
            if in_range(step - STORE_BEHIND):
                store(step - STORE_BEHIND)
